import numpy as np
import ml_dtypes


def mxq(x, axis, fmt="e4m3"):
    dtype, down = {"e4m3": (ml_dtypes.float8_e4m3fn, 7), "e5m2": (ml_dtypes.float8_e5m2, 14)}[fmt]
    v = np.moveaxis(np.asarray(x, np.float32).astype(ml_dtypes.bfloat16).astype(np.float64), axis, -1)
    blocks = v.reshape(v.shape[:-1] + (-1, 32))
    amax = np.abs(blocks).max(-1, keepdims=True)
    byte = np.maximum(np.where(amax > 0, np.frexp(amax)[1] - 1 + 127, 0) - down, 1)
    scale = np.exp2(byte - 127.0)
    codes = (blocks / scale).astype(np.float32).astype(dtype).astype(np.float64)
    return np.moveaxis((codes * scale).reshape(v.shape), -1, axis)


WIDE = False


def mx_kscale(k):
    if not WIDE:
        return np.ones(k)
    levels = np.array([20, -20, 10, -10, 0])
    a = np.random.permutation(np.resize(levels, k // 512 * 4)).reshape(k // 512, 4)
    idx = np.arange(k)
    return np.exp2(a[idx // 512, idx % 128 // 32])


BF16 = ml_dtypes.bfloat16


def bf(x):
    return np.asarray(x, np.float32).astype(BF16)


def f64(x):
    return np.asarray(x).astype(np.float64)


B, IN, OUT, G = 512, 1024, 512, 20


def silu(v):
    with np.errstate(over="ignore"):
        return v / (1.0 + np.exp(-v))


def dsilu(v):
    with np.errstate(over="ignore"):
        sg = 1.0 / (1.0 + np.exp(-v))
    return sg * (1.0 + v * (1.0 - sg))


def setup_inputs():
    bound = 1.0 / np.sqrt(IN)
    u = mx_kscale(OUT)
    x = bf(np.random.standard_normal((B, IN)))
    base_weight = np.random.uniform(-bound, bound, (OUT, IN)) / u[:, None]
    spline_weight = 0.05 * np.random.standard_normal((OUT, IN, G)) / u[:, None, None]
    spline_scale = 0.1 * (1.0 + 0.1 * np.random.standard_normal((OUT, 1, 1)))
    grid = bf(np.linspace(-2.0, 2.0, G))
    hit = np.isin(f64(x), f64(grid))
    x = bf(np.where(hit, f64(x) * (1.0 + 2.0 ** -7), f64(x)))
    g = np.random.standard_normal((B, OUT)) * np.exp2(np.random.randint(-12, 1, (B, 1))) * 8.0 * u[None, :]
    return {"x": x,
            "base_weight": bf(base_weight),
            "spline_weight": bf(spline_weight),
            "spline_scale": bf(spline_scale),
            "grid": grid,
            "grad_out": bf(g)}


def reference(x, base_weight, spline_weight, spline_scale, grid, grad_out):
    x, base_weight, spline_weight = f64(x), f64(base_weight), f64(spline_weight)
    spline_scale, grid = f64(spline_scale), f64(grid)
    nb, ni = x.shape
    no = base_weight.shape[0]
    ng = grid.shape[0]
    gq = mxq(f64(grad_out), 1, "e5m2")
    d_act = gq @ mxq(base_weight, 0, "e4m3")
    scaled_w = spline_weight * spline_scale
    w_f = scaled_w.reshape(no, ni * ng)
    d_basis = (gq @ mxq(w_f, 0, "e4m3")).reshape(nb, ni, ng)
    mask = (x[:, :, None] > grid[None, None, :]).astype(np.float64)
    return d_act * dsilu(x) + (d_basis * mask).sum(axis=2)

@@ -1,0 +1,264 @@
+from contextlib import ExitStack
+
+import concourse.mybir as mybir
+from concourse.masks import make_identity
+
+BF16 = mybir.dt.bfloat16
+F32 = mybir.dt.float32
+U32 = mybir.dt.uint32
+U8 = mybir.dt.uint8
+E4M3X4 = mybir.dt.float8_e4m3fn_x4
+E5M2X4 = mybir.dt.float8_e5m2_x4
+ALU = mybir.AluOpType
+ACT = mybir.ActivationFunctionType
+
+P = 128
+B, IN, OUT, G = 512, 1024, 512, 20
+PACK = 4
+FLOPS = 2 * B * OUT * (IN + IN * G)
+
+NT = IN // P
+NBT = B // P
+CH = P * G
+GU = 4
+UPT = G // GU
+NPASS = G + 1
+RND = 3
+RPT = NPASS // RND
+NR = NT * RPT
+LA_SC = 12
+LA_RG = 5
+
+
+def tile_relukanlayer_kernel(tc, x, base_weight, spline_weight, spline_scale, grid, grad_out, out):
+    nc = tc.nc
+    with ExitStack() as ctx:
+        const = ctx.enter_context(tc.tile_pool(name="const", bufs=1))
+        rawp = ctx.enter_context(tc.tile_pool(name="rawp", bufs=4))
+        grpp = ctx.enter_context(tc.tile_pool(name="grpp", bufs=4))
+        cdp = ctx.enter_context(tc.tile_pool(name="cdp", bufs=4))
+        tp = ctx.enter_context(tc.tile_pool(name="tp", bufs=8))
+        wkp = ctx.enter_context(tc.tile_pool(name="wkp", bufs=2))
+        osp = ctx.enter_context(tc.tile_pool(name="osp", bufs=2))
+        dps = ctx.enter_context(tc.psum_pool(name="dps", bufs=6))
+        accp = ctx.enter_context(tc.psum_pool(name="accp", bufs=2))
+        ctx.enter_context(tc.manual_schedule())
+
+        w_view = spline_weight.rearrange("(p j) i g -> p j (i g)", j=PACK)
+        out_view = out.rearrange("(t p) i -> p t i", p=P)
+
+        raws = {}
+        codes = {}
+        planes = {}
+        d_tiles = {}
+        t_tiles = {}
+        accs = {}
+
+        def load_chunk(c):
+            raw = rawp.tile([P, PACK, CH], BF16, name="raw")
+            raws[c] = raw
+            for j in range(PACK):
+                nc.sync.dma_start(out=raw[:, j, :], in_=w_view[:, j, c * CH:(c + 1) * CH])
+
+        s_bf = const.tile([P, PACK], BF16, name="s_bf")
+        nc.scalar.dma_start(out=s_bf[:], in_=spline_scale.rearrange("(p j) a c -> p (j a c)", j=PACK))
+        grid_bf = const.tile([P, G], BF16, name="grid_bf")
+        nc.scalar.dma_start(out=grid_bf[:], in_=grid.partition_broadcast(P))
+        x_sb = const.tile([P, NBT, IN], BF16, name="x_sb")
+        nc.sync.dma_start(out=x_sb[:], in_=x.rearrange("(t p) i -> p t i", p=P))
+        g_sb = const.tile([P, NBT, OUT], BF16, name="g_sb")
+        nc.sync.dma_start(out=g_sb[:], in_=grad_out.rearrange("(t p) o -> p t o", p=P))
+        load_chunk(0)
+        rawb = const.tile([P, PACK, IN], BF16, name="rawb")
+        nc.sync.dma_start(out=rawb[:], in_=base_weight.rearrange("(p j) i -> p j i", j=PACK))
+        load_chunk(1)
+        load_chunk(2)
+        load_chunk(3)
+
+        ident_b = const.tile([P, P], BF16, name="ident_b")
+        make_identity(nc, ident_b[:])
+        ident_f = const.tile([P, P], F32, name="ident_f")
+        make_identity(nc, ident_f[:])
+
+        s32 = const.tile([P, PACK], F32, name="s32")
+        nc.vector.tensor_copy(out=s32[:], in_=s_bf[:])
+        grid32 = const.tile([P, G], F32, name="grid32")
+        nc.vector.tensor_copy(out=grid32[:], in_=grid_bf[:])
+
+        xT = const.tile([P, NT, B], BF16, name="xT")
+        sg = const.tile([P, NT, B], F32, name="sg")
+        nds = const.tile([P, NT, B], F32, name="nds")
+
+        def x_transposes(k):
+            xp = dps.tile([P, 2, B], BF16, tag="d", name="xp")
+            for h in range(2):
+                for t in range(NBT):
+                    nc.tensor.transpose(
+                        xp[:, h, t * P:(t + 1) * P], x_sb[:, t, (2 * k + h) * P:(2 * k + h + 1) * P], ident_b[:]
+                    )
+            nc.vector.tensor_copy(out=xT[:, 2 * k:2 * k + 2, :], in_=xp[:])
+            nc.scalar.activation(out=sg[:, 2 * k:2 * k + 2, :], in_=xT[:, 2 * k:2 * k + 2, :], func=ACT.Sigmoid)
+
+        def dsilu(k):
+            sl = slice(2 * k, 2 * k + 2)
+            tq = wkp.tile([P, 2, B], F32, name="tq")
+            nc.vector.scalar_tensor_tensor(
+                out=tq[:], in0=sg[:, sl, :], scalar=1.0, in1=xT[:, sl, :], op0=ALU.subtract, op1=ALU.mult
+            )
+            nc.vector.scalar_tensor_tensor(
+                out=nds[:, sl, :], in0=tq[:], scalar=1.0, in1=sg[:, sl, :], op0=ALU.subtract, op1=ALU.mult
+            )
+
+        gg = const.tile([P, PACK * B], BF16, name="gg", align_bytes=64)
+        gq_c = const.tile([P, B], U32, name="gq_c", align_bytes=64)
+        gq_s = const.tile([P, B], U8, name="gq_s", align_bytes=64)
+
+        def g_transposes():
+            for h in range(2):
+                gp = dps.tile([P, 2, 2 * P], F32, tag="d", name="gp")
+                for u in range(2):
+                    for tt in range(2):
+                        words = g_sb[:, 2 * h + tt, :].bitcast(F32).rearrange("p (q u) -> p q u", u=2)[:, :, u]
+                        nc.tensor.transpose(gp[:, u, tt * P:(tt + 1) * P], words, ident_f[:])
+                nc.scalar.copy(
+                    out=gg[:].bitcast(F32)[:, h * 4 * P:(h + 1) * 4 * P].rearrange("p (b u) -> p b u", u=2),
+                    in_=gp[:].rearrange("p u b -> p b u"),
+                )
+
+        def scale_chunk(c, eng):
+            raw = raws[c]
+            for j in range(PACK):
+                if eng == "v":
+                    nc.vector.tensor_scalar(
+                        out=raw[:, j, :], in0=raw[:, j, :], scalar1=s32[:, j:j + 1], scalar2=None, op0=ALU.mult
+                    )
+                else:
+                    nc.gpsimd.tensor_scalar(
+                        out=raw[:, j, :], in0=raw[:, j, :], scalar1=s32[:, j:j + 1], scalar2=0.0,
+                        op0=ALU.mult, op1=ALU.add,
+                    )
+
+        grps = {}
+
+        def regroup(u):
+            it, q = divmod(u, UPT)
+            grp = grpp.tile([P, GU * P * PACK], BF16, name="grp", align_bytes=64)
+            grps[u] = grp
+            src = raws[it][:].rearrange("p j (i g) -> p i j g", g=G)[:, :, :, q * GU:(q + 1) * GU]
+            dst = grp[:].rearrange("p (g i j) -> p i j g", g=GU, j=PACK)
+            nc.scalar.copy(out=dst, in_=src)
+
+        def quantise(u):
+            cd = cdp.tile([P, GU * P], U32, name="cd", align_bytes=64)
+            pl = cdp.tile([P, GU * P], U8, name="pl", align_bytes=64)
+            codes[u] = cd
+            planes[u] = pl
+            nc.vector.quantize_mx(out=cd[:].bitcast(E4M3X4), scales=pl[:], in_=grps[u][:])
+
+        bgrp = const.tile([P, IN * PACK], BF16, name="bgrp", align_bytes=64)
+        b_c = const.tile([P, IN], U32, name="b_c", align_bytes=64)
+        b_s = const.tile([P, IN], U8, name="b_s", align_bytes=64)
+
+        def base_regroup():
+            nc.gpsimd.tensor_scalar(
+                out=bgrp[:].rearrange("p (w j) -> p w j", j=PACK), in0=rawb[:].rearrange("p j w -> p w j"),
+                scalar1=1.0, scalar2=0.0, op0=ALU.mult, op1=ALU.add,
+            )
+
+        def base_quantise():
+            nc.vector.quantize_mx(out=b_c[:].bitcast(E4M3X4), scales=b_s[:], in_=bgrp[:])
+
+        def mx_round(r):
+            for n in range(RND * r, RND * r + RND):
+                it, s = divmod(n, NPASS)
+                d = dps.tile([P, B], F32, tag="d", name="d")
+                d_tiles[n] = d
+                if s < G:
+                    u = it * UPT + s // GU
+                    cols = slice((s % GU) * P, (s % GU + 1) * P)
+                    lhsT, lhsT_scale = codes[u][:, cols], planes[u][:, cols]
+                else:
+                    cols = slice(it * P, (it + 1) * P)
+                    lhsT, lhsT_scale = b_c[:, cols], b_s[:, cols]
+                nc.tensor.matmul_mx(
+                    out=d[:], lhsT=lhsT.bitcast(E4M3X4), lhsT_scale=lhsT_scale,
+                    rhs=gq_c[:].bitcast(E5M2X4), rhs_scale=gq_s[:], start=True, stop=True,
+                )
+
+        def t3_round(r):
+            for n in range(RND * r, RND * r + RND):
+                it, s = divmod(n, NPASS)
+                t = tp.tile([P, B], F32, name="t")
+                t_tiles[n] = t
+                if s < G:
+                    nc.vector.scalar_tensor_tensor(
+                        out=t[:], in0=xT[:, it, :], scalar=grid32[:, s:s + 1], in1=d_tiles[n][:],
+                        op0=ALU.is_gt, op1=ALU.mult,
+                    )
+                else:
+                    nc.vector.scalar_tensor_tensor(
+                        out=t[:], in0=nds[:, it, :], scalar=-1.0, in1=d_tiles[n][:], op0=ALU.mult, op1=ALU.mult
+                    )
+
+        def tr_round(r):
+            for n in range(RND * r, RND * r + RND):
+                it, s = divmod(n, NPASS)
+                if s == 0:
+                    acc = accp.tile([P, B], F32, name="acc")
+                    accs[it] = acc
+                for bt in range(NBT):
+                    nc.tensor.matmul(
+                        out=accs[it][:, bt * P:(bt + 1) * P], lhsT=t_tiles[n][:, bt * P:(bt + 1) * P], rhs=ident_f[:],
+                        is_transpose=True, start=(s == 0 and bt == 0), stop=(s == NPASS - 1 and bt == NBT - 1),
+                    )
+
+        def evacuate(it):
+            osb = osp.tile([P, NBT, P], F32, name="osb")
+            nc.scalar.copy(out=osb[:].rearrange("p t i -> p (t i)"), in_=accs[it][:])
+            nc.sync.dma_start(out=out_view[:, :, it * P:(it + 1) * P], in_=osb[:])
+
+        def first_round(u):
+            it, q = divmod(u, UPT)
+            return it * RPT + (q * GU) // RND
+
+        x_transposes(0)
+        x_transposes(1)
+        g_transposes()
+        x_transposes(2)
+        x_transposes(3)
+        base_regroup()
+        scale_chunk(0, "v")
+        dsilu(0)
+        dsilu(1)
+        nc.vector.quantize_mx(out=gq_c[:].bitcast(E5M2X4), scales=gq_s[:], in_=gg[:])
+        dsilu(2)
+        regroup(0)
+        quantise(0)
+
+        nxt = {"sc": 1, "rg": 1, "q": 1}
+        for r in range(NR + 1):
+            while nxt["sc"] < NT and nxt["sc"] * RPT - LA_SC <= r:
+                scale_chunk(nxt["sc"], "g")
+                nxt["sc"] += 1
+            while nxt["rg"] < NT * UPT and first_round(nxt["rg"]) - LA_RG <= r:
+                u = nxt["rg"]
+                regroup(u)
+                if u % UPT == UPT - 1 and u // UPT + 4 < NT:
+                    load_chunk(u // UPT + 4)
+                nxt["rg"] += 1
+            if r < NR:
+                mx_round(r)
+            if r >= 1:
+                tr_round(r - 1)
+            if r < NR:
+                t3_round(r)
+            ahead = 1 if r < 4 else 2
+            while nxt["q"] < NT * UPT and first_round(nxt["q"]) <= r + ahead:
+                quantise(nxt["q"])
+                nxt["q"] += 1
+            if r == 2:
+                dsilu(3)
+            if r == 3:
+                base_quantise()
+            if r >= 1 and (r - 1) % RPT == RPT - 1:
+                evacuate((r - 1) // RPT)

@@ -238,7 +238,7 @@ def tile_relukanlayer_kernel(tc, x, base_weight, spline_weight, spline_scale, gr
         nxt = {"sc": 1, "rg": 1, "q": 1}
         for r in range(NR + 1):
             while nxt["sc"] < NT and nxt["sc"] * RPT - LA_SC <= r:
-                scale_chunk(nxt["sc"], "g")
+                scale_chunk(nxt["sc"], "v")
                 nxt["sc"] += 1
             while nxt["rg"] < NT * UPT and first_round(nxt["rg"]) - LA_RG <= r:
                 u = nxt["rg"]

@@ -26,8 +26,8 @@ NPASS = G + 1
 RND = 3
 RPT = NPASS // RND
 NR = NT * RPT
-LA_SC = 12
-LA_RG = 5
+LA_RG = 4
+V_CHUNKS = 3
 
 
 def tile_relukanlayer_kernel(tc, x, base_weight, spline_weight, spline_scale, grid, grad_out, out):
@@ -35,10 +35,11 @@ def tile_relukanlayer_kernel(tc, x, base_weight, spline_weight, spline_scale, gr
     with ExitStack() as ctx:
         const = ctx.enter_context(tc.tile_pool(name="const", bufs=1))
         rawp = ctx.enter_context(tc.tile_pool(name="rawp", bufs=4))
-        grpp = ctx.enter_context(tc.tile_pool(name="grpp", bufs=4))
+        grpp = ctx.enter_context(tc.tile_pool(name="grpp", bufs=3))
         cdp = ctx.enter_context(tc.tile_pool(name="cdp", bufs=4))
         tp = ctx.enter_context(tc.tile_pool(name="tp", bufs=8))
-        wkp = ctx.enter_context(tc.tile_pool(name="wkp", bufs=2))
+        wkp = ctx.enter_context(tc.tile_pool(name="wkp", bufs=1))
+        flp = ctx.enter_context(tc.tile_pool(name="flp", bufs=2))
         osp = ctx.enter_context(tc.tile_pool(name="osp", bufs=2))
         dps = ctx.enter_context(tc.psum_pool(name="dps", bufs=6))
         accp = ctx.enter_context(tc.psum_pool(name="accp", bufs=2))
@@ -96,7 +97,7 @@ def tile_relukanlayer_kernel(tc, x, base_weight, spline_weight, spline_scale, gr
                     nc.tensor.transpose(
                         xp[:, h, t * P:(t + 1) * P], x_sb[:, t, (2 * k + h) * P:(2 * k + h + 1) * P], ident_b[:]
                     )
-            nc.vector.tensor_copy(out=xT[:, 2 * k:2 * k + 2, :], in_=xp[:])
+            nc.scalar.copy(out=xT[:, 2 * k:2 * k + 2, :], in_=xp[:])
             nc.scalar.activation(out=sg[:, 2 * k:2 * k + 2, :], in_=xT[:, 2 * k:2 * k + 2, :], func=ACT.Sigmoid)
 
         def dsilu(k):
@@ -125,35 +126,61 @@ def tile_relukanlayer_kernel(tc, x, base_weight, spline_weight, spline_scale, gr
                     in_=gp[:].rearrange("p u b -> p b u"),
                 )
 
-        def scale_chunk(c, eng):
+        def scale_v(c):
             raw = raws[c]
             for j in range(PACK):
-                if eng == "v":
-                    nc.vector.tensor_scalar(
-                        out=raw[:, j, :], in0=raw[:, j, :], scalar1=s32[:, j:j + 1], scalar2=None, op0=ALU.mult
-                    )
-                else:
-                    nc.gpsimd.tensor_scalar(
-                        out=raw[:, j, :], in0=raw[:, j, :], scalar1=s32[:, j:j + 1], scalar2=0.0,
-                        op0=ALU.mult, op1=ALU.add,
-                    )
+                nc.vector.tensor_scalar(
+                    out=raw[:, j, :], in0=raw[:, j, :], scalar1=s32[:, j:j + 1], scalar2=None, op0=ALU.mult
+                )
 
+        def scale_g(c, js):
+            raw = raws[c]
+            fl = flp.tile([P, 1], F32, name="fl")
+            nc.vector.memset(fl[:], 0.0)
+            for j in js:
+                nc.gpsimd.tensor_scalar(
+                    out=raw[:, j, :], in0=raw[:, j, :], scalar1=s32[:, j:j + 1],
+                    scalar2=(fl[:, 0:1] if j == js[0] else 0.0), op0=ALU.mult, op1=ALU.add,
+                )
+
+        groups = [(u, 1) for u in range(UPT)]
+        for c in range(1, NT):
+            groups.extend([(c * UPT, 2), (c * UPT + 2, 2), (c * UPT + 4, 1)])
+        group_of = {}
+        for k, (u0, nu) in enumerate(groups):
+            for u in range(u0, u0 + nu):
+                group_of[u] = k
+        UW = GU * P
         grps = {}
+        done_rg = set()
 
         def regroup(u):
             it, q = divmod(u, UPT)
-            grp = grpp.tile([P, GU * P * PACK], BF16, name="grp", align_bytes=64)
-            grps[u] = grp
+            k = group_of[u]
+            if u == groups[k][0]:
+                grp = grpp.tile([P, 2 * UW * PACK], BF16, name="grp", align_bytes=64)
+                grps[k] = grp
+            off = (u - groups[k][0]) * UW * PACK
             src = raws[it][:].rearrange("p j (i g) -> p i j g", g=G)[:, :, :, q * GU:(q + 1) * GU]
-            dst = grp[:].rearrange("p (g i j) -> p i j g", g=GU, j=PACK)
+            dst = grps[k][:, off:off + UW * PACK].rearrange("p (g i j) -> p i j g", g=GU, j=PACK)
             nc.scalar.copy(out=dst, in_=src)
+            done_rg.add(u)
 
-        def quantise(u):
-            cd = cdp.tile([P, GU * P], U32, name="cd", align_bytes=64)
-            pl = cdp.tile([P, GU * P], U8, name="pl", align_bytes=64)
-            codes[u] = cd
-            planes[u] = pl
-            nc.vector.quantize_mx(out=cd[:].bitcast(E4M3X4), scales=pl[:], in_=grps[u][:])
+        def quantise(k):
+            u0, nu = groups[k]
+            assert all(u in done_rg for u in range(u0, u0 + nu))
+            cd = cdp.tile([P, 2 * UW], U32, name="cd", align_bytes=64)
+            pl = cdp.tile([P, 2 * UW], U8, name="pl", align_bytes=64)
+            codes[k] = cd
+            planes[k] = pl
+            nc.vector.quantize_mx(
+                out=cd[:, 0:nu * UW].bitcast(E4M3X4), scales=pl[:, 0:nu * UW], in_=grps[k][:, 0:nu * UW * PACK]
+            )
+            c, q = divmod(u0, UPT)
+            if q == 2 and V_CHUNKS <= c + 2 < NT:
+                scale_g(c + 2, [0, 1])
+            if q == 0 and V_CHUNKS <= c + 1 < NT:
+                scale_g(c + 1, [2, 3])
 
         bgrp = const.tile([P, IN * PACK], BF16, name="bgrp", align_bytes=64)
         b_c = const.tile([P, IN], U32, name="b_c", align_bytes=64)
@@ -175,8 +202,10 @@ def tile_relukanlayer_kernel(tc, x, base_weight, spline_weight, spline_scale, gr
                 d_tiles[n] = d
                 if s < G:
                     u = it * UPT + s // GU
-                    cols = slice((s % GU) * P, (s % GU + 1) * P)
-                    lhsT, lhsT_scale = codes[u][:, cols], planes[u][:, cols]
+                    k = group_of[u]
+                    c0 = (u - groups[k][0]) * UW + (s % GU) * P
+                    cols = slice(c0, c0 + P)
+                    lhsT, lhsT_scale = codes[k][:, cols], planes[k][:, cols]
                 else:
                     cols = slice(it * P, (it + 1) * P)
                     lhsT, lhsT_scale = b_c[:, cols], b_s[:, cols]
@@ -221,13 +250,24 @@ def tile_relukanlayer_kernel(tc, x, base_weight, spline_weight, spline_scale, gr
             it, q = divmod(u, UPT)
             return it * RPT + (q * GU) // RND
 
+        def slot(k):
+            u0 = groups[k][0]
+            if u0 < 3:
+                return first_round(u0) - 1
+            return first_round(u0) - 2 - (1 if u0 % UPT == 0 and u0 >= 2 * UPT else 0)
+
+        def last_group(r):
+            n = min(RND * r + RND - 1, NT * NPASS - 1)
+            it, s = divmod(n, NPASS)
+            return group_of[it * UPT + min(s, G - 1) // GU]
+
         x_transposes(0)
         x_transposes(1)
         g_transposes()
         x_transposes(2)
         x_transposes(3)
         base_regroup()
-        scale_chunk(0, "v")
+        scale_v(0)
         dsilu(0)
         dsilu(1)
         nc.vector.quantize_mx(out=gq_c[:].bitcast(E5M2X4), scales=gq_s[:], in_=gg[:])
@@ -235,27 +275,31 @@ def tile_relukanlayer_kernel(tc, x, base_weight, spline_weight, spline_scale, gr
         regroup(0)
         quantise(0)
 
-        nxt = {"sc": 1, "rg": 1, "q": 1}
-        for r in range(NR + 1):
-            while nxt["sc"] < NT and nxt["sc"] * RPT - LA_SC <= r:
-                scale_chunk(nxt["sc"], "v")
-                nxt["sc"] += 1
+        nxt = {"rg": 1, "q": 1}
+        for r in range(-1, NR + 1):
+            for c in range(1, V_CHUNKS):
+                if r == 6 * c - 4:
+                    scale_v(c)
             while nxt["rg"] < NT * UPT and first_round(nxt["rg"]) - LA_RG <= r:
                 u = nxt["rg"]
                 regroup(u)
                 if u % UPT == UPT - 1 and u // UPT + 4 < NT:
                     load_chunk(u // UPT + 4)
                 nxt["rg"] += 1
-            if r < NR:
-                mx_round(r)
+            early = r + 1 < NR and last_group(r + 1) < nxt["q"]
+            if early:
+                mx_round(r + 1)
             if r >= 1:
                 tr_round(r - 1)
-            if r < NR:
+            if 0 <= r < NR:
                 t3_round(r)
-            ahead = 1 if r < 4 else 2
-            while nxt["q"] < NT * UPT and first_round(nxt["q"]) <= r + ahead:
+            while nxt["q"] < len(groups) and (
+                slot(nxt["q"]) <= r or (r + 1 < NR and nxt["q"] <= last_group(r + 1))
+            ):
                 quantise(nxt["q"])
                 nxt["q"] += 1
+            if r + 1 < NR and not early:
+                mx_round(r + 1)
             if r == 2:
                 dsilu(3)
             if r == 3:

@@ -100,14 +100,20 @@ def tile_relukanlayer_kernel(tc, x, base_weight, spline_weight, spline_scale, gr
             nc.scalar.copy(out=xT[:, 2 * k:2 * k + 2, :], in_=xp[:])
             nc.scalar.activation(out=sg[:, 2 * k:2 * k + 2, :], in_=xT[:, 2 * k:2 * k + 2, :], func=ACT.Sigmoid)
 
-        def dsilu(k):
+        tqs = {}
+
+        def dsilu_a(k):
             sl = slice(2 * k, 2 * k + 2)
             tq = wkp.tile([P, 2, B], F32, name="tq")
+            tqs[k] = tq
             nc.vector.scalar_tensor_tensor(
                 out=tq[:], in0=sg[:, sl, :], scalar=1.0, in1=xT[:, sl, :], op0=ALU.subtract, op1=ALU.mult
             )
+
+        def dsilu_b(k):
+            sl = slice(2 * k, 2 * k + 2)
             nc.vector.scalar_tensor_tensor(
-                out=nds[:, sl, :], in0=tq[:], scalar=1.0, in1=sg[:, sl, :], op0=ALU.subtract, op1=ALU.mult
+                out=nds[:, sl, :], in0=tqs[k][:], scalar=1.0, in1=sg[:, sl, :], op0=ALU.subtract, op1=ALU.mult
             )
 
         gg = const.tile([P, PACK * B], BF16, name="gg", align_bytes=64)
@@ -126,9 +132,9 @@ def tile_relukanlayer_kernel(tc, x, base_weight, spline_weight, spline_scale, gr
                     in_=gp[:].rearrange("p u b -> p b u"),
                 )
 
-        def scale_v(c):
+        def scale_v(c, js):
             raw = raws[c]
-            for j in range(PACK):
+            for j in js:
                 nc.vector.tensor_scalar(
                     out=raw[:, j, :], in0=raw[:, j, :], scalar1=s32[:, j:j + 1], scalar2=None, op0=ALU.mult
                 )
@@ -161,8 +167,8 @@ def tile_relukanlayer_kernel(tc, x, base_weight, spline_weight, spline_scale, gr
                 grp = grpp.tile([P, 2 * UW * PACK], BF16, name="grp", align_bytes=64)
                 grps[k] = grp
             off = (u - groups[k][0]) * UW * PACK
-            src = raws[it][:].rearrange("p j (i g) -> p i j g", g=G)[:, :, :, q * GU:(q + 1) * GU]
-            dst = grps[k][:, off:off + UW * PACK].rearrange("p (g i j) -> p i j g", g=GU, j=PACK)
+            src = raws[it][:].rearrange("p j (i g) -> p i g j", g=G)[:, :, q * GU:(q + 1) * GU, :]
+            dst = grps[k][:, off:off + UW * PACK].rearrange("p (g i j) -> p i g j", g=GU, j=PACK)
             nc.scalar.copy(out=dst, in_=src)
             done_rg.add(u)
 
@@ -267,11 +273,17 @@ def tile_relukanlayer_kernel(tc, x, base_weight, spline_weight, spline_scale, gr
         x_transposes(2)
         x_transposes(3)
         base_regroup()
-        scale_v(0)
-        dsilu(0)
-        dsilu(1)
+        scale_v(0, [0])
+        dsilu_a(0)
+        scale_v(0, [1])
+        dsilu_b(0)
+        scale_v(0, [2])
+        dsilu_a(1)
+        scale_v(0, [3])
+        dsilu_b(1)
         nc.vector.quantize_mx(out=gq_c[:].bitcast(E5M2X4), scales=gq_s[:], in_=gg[:])
-        dsilu(2)
+        dsilu_a(2)
+        dsilu_b(2)
         regroup(0)
         quantise(0)
 
@@ -279,7 +291,7 @@ def tile_relukanlayer_kernel(tc, x, base_weight, spline_weight, spline_scale, gr
         for r in range(-1, NR + 1):
             for c in range(1, V_CHUNKS):
                 if r == 6 * c - 4:
-                    scale_v(c)
+                    scale_v(c, [0, 1, 2, 3])
             while nxt["rg"] < NT * UPT and first_round(nxt["rg"]) - LA_RG <= r:
                 u = nxt["rg"]
                 regroup(u)
@@ -301,7 +313,8 @@ def tile_relukanlayer_kernel(tc, x, base_weight, spline_weight, spline_scale, gr
             if r + 1 < NR and not early:
                 mx_round(r + 1)
             if r == 2:
-                dsilu(3)
+                dsilu_a(3)
+                dsilu_b(3)
             if r == 3:
                 base_quantise()
             if r >= 1 and (r - 1) % RPT == RPT - 1:

@@ -139,14 +139,14 @@ def tile_relukanlayer_kernel(tc, x, base_weight, spline_weight, spline_scale, gr
                     out=raw[:, j, :], in0=raw[:, j, :], scalar1=s32[:, j:j + 1], scalar2=None, op0=ALU.mult
                 )
 
-        def scale_g(c, js):
+        def scale_g(c, pieces):
             raw = raws[c]
             fl = flp.tile([P, 1], F32, name="fl")
             nc.vector.memset(fl[:], 0.0)
-            for j in js:
+            for n, (j, lo, hi) in enumerate(pieces):
                 nc.gpsimd.tensor_scalar(
-                    out=raw[:, j, :], in0=raw[:, j, :], scalar1=s32[:, j:j + 1],
-                    scalar2=(fl[:, 0:1] if j == js[0] else 0.0), op0=ALU.mult, op1=ALU.add,
+                    out=raw[:, j, lo:hi], in0=raw[:, j, lo:hi], scalar1=s32[:, j:j + 1],
+                    scalar2=(fl[:, 0:1] if n == 0 else 0.0), op0=ALU.mult, op1=ALU.add,
                 )
 
         groups = [(u, 1) for u in range(UPT)]
@@ -179,14 +179,25 @@ def tile_relukanlayer_kernel(tc, x, base_weight, spline_weight, spline_scale, gr
             pl = cdp.tile([P, 2 * UW], U8, name="pl", align_bytes=64)
             codes[k] = cd
             planes[k] = pl
-            nc.vector.quantize_mx(
-                out=cd[:, 0:nu * UW].bitcast(E4M3X4), scales=pl[:, 0:nu * UW], in_=grps[k][:, 0:nu * UW * PACK]
-            )
             c, q = divmod(u0, UPT)
+            window = None
             if q == 2 and V_CHUNKS <= c + 2 < NT:
-                scale_g(c + 2, [0, 1])
+                window = (c + 2, [(0, 0, CH), (1, 0, CH // 2)])
             if q == 0 and V_CHUNKS <= c + 1 < NT:
-                scale_g(c + 1, [2, 3])
+                window = (c + 1, [(1, CH // 2, CH), (2, 0, CH)])
+                scale_v(c + 1, [3])
+            if window is None:
+                nc.vector.quantize_mx(
+                    out=cd[:, 0:nu * UW].bitcast(E4M3X4), scales=pl[:, 0:nu * UW], in_=grps[k][:, 0:nu * UW * PACK]
+                )
+            else:
+                for h in range(2):
+                    nc.vector.quantize_mx(
+                        out=cd[:, h * UW:(h + 1) * UW].bitcast(E4M3X4), scales=pl[:, h * UW:(h + 1) * UW],
+                        in_=grps[k][:, h * UW * PACK:(h + 1) * UW * PACK],
+                    )
+                    if h == 0:
+                        scale_g(window[0], window[1])
 
         bgrp = const.tile([P, IN * PACK], BF16, name="bgrp", align_bytes=64)
         b_c = const.tile([P, IN], U32, name="b_c", align_bytes=64)

@@ -23,10 +23,7 @@ CH = P * G
 GU = 4
 UPT = G // GU
 NPASS = G + 1
-RND = 3
-RPT = NPASS // RND
-NR = NT * RPT
-LA_RG = 4
+RND = 6
 V_CHUNKS = 3
 
 
@@ -213,7 +210,7 @@ def tile_relukanlayer_kernel(tc, x, base_weight, spline_weight, spline_scale, gr
             nc.vector.quantize_mx(out=b_c[:].bitcast(E4M3X4), scales=b_s[:], in_=bgrp[:])
 
         def mx_round(r):
-            for n in range(RND * r, RND * r + RND):
+            for n in range(rounds[r][0], rounds[r][1]):
                 it, s = divmod(n, NPASS)
                 d = dps.tile([P, B], F32, tag="d", name="d")
                 d_tiles[n] = d
@@ -231,23 +228,22 @@ def tile_relukanlayer_kernel(tc, x, base_weight, spline_weight, spline_scale, gr
                     rhs=gq_c[:].bitcast(E5M2X4), rhs_scale=gq_s[:], start=True, stop=True,
                 )
 
-        def t3_round(r):
-            for n in range(RND * r, RND * r + RND):
-                it, s = divmod(n, NPASS)
-                t = tp.tile([P, B], F32, name="t")
-                t_tiles[n] = t
-                if s < G:
-                    nc.vector.scalar_tensor_tensor(
-                        out=t[:], in0=xT[:, it, :], scalar=grid32[:, s:s + 1], in1=d_tiles[n][:],
-                        op0=ALU.is_gt, op1=ALU.mult,
-                    )
-                else:
-                    nc.vector.scalar_tensor_tensor(
-                        out=t[:], in0=nds[:, it, :], scalar=-1.0, in1=d_tiles[n][:], op0=ALU.mult, op1=ALU.mult
-                    )
+        def mask(n):
+            it, s = divmod(n, NPASS)
+            t = tp.tile([P, B], F32, name="t")
+            t_tiles[n] = t
+            if s < G:
+                nc.vector.scalar_tensor_tensor(
+                    out=t[:], in0=xT[:, it, :], scalar=grid32[:, s:s + 1], in1=d_tiles[n][:],
+                    op0=ALU.is_gt, op1=ALU.mult,
+                )
+            else:
+                nc.vector.scalar_tensor_tensor(
+                    out=t[:], in0=nds[:, it, :], scalar=-1.0, in1=d_tiles[n][:], op0=ALU.mult, op1=ALU.mult
+                )
 
         def tr_round(r):
-            for n in range(RND * r, RND * r + RND):
+            for n in range(rounds[r][0], rounds[r][1]):
                 it, s = divmod(n, NPASS)
                 if s == 0:
                     acc = accp.tile([P, B], F32, name="acc")
@@ -263,20 +259,27 @@ def tile_relukanlayer_kernel(tc, x, base_weight, spline_weight, spline_scale, gr
             nc.scalar.copy(out=osb[:].rearrange("p t i -> p (t i)"), in_=accs[it][:])
             nc.sync.dma_start(out=out_view[:, :, it * P:(it + 1) * P], in_=osb[:])
 
-        def first_round(u):
+        def first_pass(u):
             it, q = divmod(u, UPT)
-            return it * RPT + (q * GU) // RND
+            return it * NPASS + q * GU
 
-        def slot(k):
+        NP = NT * NPASS
+        rounds = [(0, 4), (4, 8), (8, 12), (12, 16), (16, NPASS)]
+        rounds.extend([(a, min(a + RND, NP)) for a in range(NPASS, NP, RND)])
+
+        def quantise_after(k):
             u0 = groups[k][0]
-            if u0 < 3:
-                return first_round(u0) - 1
-            return first_round(u0) - 2 - (1 if u0 % UPT == 0 and u0 >= 2 * UPT else 0)
+            c, q = divmod(u0, UPT)
+            if c == 0:
+                return first_pass(u0) - 1
+            if c == 1:
+                return first_pass(u0) - (3 if q == 0 else 7)
+            return first_pass(u0) - (10 - q // 2)
 
-        def last_group(r):
-            n = min(RND * r + RND - 1, NT * NPASS - 1)
-            it, s = divmod(n, NPASS)
-            return group_of[it * UPT + min(s, G - 1) // GU]
+        def regroup_after(u):
+            if u < UPT:
+                return first_pass(u) - 12
+            return first_pass(u) - (13 if u < 2 * UPT else 15)
 
         x_transposes(0)
         x_transposes(1)
@@ -299,34 +302,38 @@ def tile_relukanlayer_kernel(tc, x, base_weight, spline_weight, spline_scale, gr
         quantise(0)
 
         nxt = {"rg": 1, "q": 1}
-        for r in range(-1, NR + 1):
-            for c in range(1, V_CHUNKS):
-                if r == 6 * c - 4:
-                    scale_v(c, [0, 1, 2, 3])
-            while nxt["rg"] < NT * UPT and first_round(nxt["rg"]) - LA_RG <= r:
+
+        def after_pass(n):
+            if n == 8:
+                scale_v(1, [0, 1, 2, 3])
+                dsilu_a(3)
+                dsilu_b(3)
+            if n == 11:
+                base_quantise()
+            if n == 26:
+                scale_v(2, [0, 1, 2, 3])
+            while nxt["rg"] < NT * UPT and regroup_after(nxt["rg"]) <= n:
                 u = nxt["rg"]
                 regroup(u)
                 if u % UPT == UPT - 1 and u // UPT + 4 < NT:
                     load_chunk(u // UPT + 4)
                 nxt["rg"] += 1
-            early = r + 1 < NR and last_group(r + 1) < nxt["q"]
-            if early:
-                mx_round(r + 1)
-            if r >= 1:
-                tr_round(r - 1)
-            if 0 <= r < NR:
-                t3_round(r)
-            while nxt["q"] < len(groups) and (
-                slot(nxt["q"]) <= r or (r + 1 < NR and nxt["q"] <= last_group(r + 1))
-            ):
+            while nxt["q"] < len(groups) and quantise_after(nxt["q"]) <= n:
                 quantise(nxt["q"])
                 nxt["q"] += 1
-            if r + 1 < NR and not early:
+
+        after_pass(-1)
+        mx_round(0)
+        for r in range(len(rounds)):
+            if r >= 1:
+                tr_round(r - 1)
+                for n in range(rounds[r - 1][0], rounds[r - 1][1]):
+                    if n % NPASS == NPASS - 1:
+                        evacuate(n // NPASS)
+            for n in range(rounds[r][0], rounds[r][1]):
+                mask(n)
+                after_pass(n)
+            if r + 1 < len(rounds):
                 mx_round(r + 1)
-            if r == 2:
-                dsilu_a(3)
-                dsilu_b(3)
-            if r == 3:
-                base_quantise()
-            if r >= 1 and (r - 1) % RPT == RPT - 1:
-                evacuate((r - 1) // RPT)
+        tr_round(len(rounds) - 1)
+        evacuate(NT - 1)

@@ -23,7 +23,8 @@ CH = P * G
 GU = 4
 UPT = G // GU
 NPASS = G + 1
-RND = 6
+RND = 2
+LA = 2
 V_CHUNKS = 3
 
 
@@ -187,6 +188,8 @@ def tile_relukanlayer_kernel(tc, x, base_weight, spline_weight, spline_scale, gr
                 nc.vector.quantize_mx(
                     out=cd[:, 0:nu * UW].bitcast(E4M3X4), scales=pl[:, 0:nu * UW], in_=grps[k][:, 0:nu * UW * PACK]
                 )
+                if k < 4:
+                    base_regroup(k)
             else:
                 for h in range(2):
                     nc.vector.quantize_mx(
@@ -200,14 +203,20 @@ def tile_relukanlayer_kernel(tc, x, base_weight, spline_weight, spline_scale, gr
         b_c = const.tile([P, IN], U32, name="b_c", align_bytes=64)
         b_s = const.tile([P, IN], U8, name="b_s", align_bytes=64)
 
-        def base_regroup():
+        BW = IN // 4
+
+        def base_regroup(m):
+            fl = flp.tile([P, 1], F32, name="fl")
+            nc.vector.memset(fl[:], 0.0)
             nc.gpsimd.tensor_scalar(
-                out=bgrp[:].rearrange("p (w j) -> p w j", j=PACK), in0=rawb[:].rearrange("p j w -> p w j"),
-                scalar1=1.0, scalar2=0.0, op0=ALU.mult, op1=ALU.add,
+                out=bgrp[:, m * BW * PACK:(m + 1) * BW * PACK].rearrange("p (w j) -> p w j", j=PACK),
+                in0=rawb[:, :, m * BW:(m + 1) * BW].rearrange("p j w -> p w j"),
+                scalar1=1.0, scalar2=fl[:, 0:1], op0=ALU.mult, op1=ALU.add,
             )
 
         def base_quantise():
             nc.vector.quantize_mx(out=b_c[:].bitcast(E4M3X4), scales=b_s[:], in_=bgrp[:])
+            done_rg.add("base")
 
         def mx_round(r):
             for n in range(rounds[r][0], rounds[r][1]):
@@ -264,8 +273,7 @@ def tile_relukanlayer_kernel(tc, x, base_weight, spline_weight, spline_scale, gr
             return it * NPASS + q * GU
 
         NP = NT * NPASS
-        rounds = [(0, 4), (4, 8), (8, 12), (12, 16), (16, NPASS)]
-        rounds.extend([(a, min(a + RND, NP)) for a in range(NPASS, NP, RND)])
+        rounds = [(a, a + RND) for a in range(0, NP, RND)]
 
         def quantise_after(k):
             u0 = groups[k][0]
@@ -286,7 +294,6 @@ def tile_relukanlayer_kernel(tc, x, base_weight, spline_weight, spline_scale, gr
         g_transposes()
         x_transposes(2)
         x_transposes(3)
-        base_regroup()
         scale_v(0, [0])
         dsilu_a(0)
         scale_v(0, [1])
@@ -301,17 +308,9 @@ def tile_relukanlayer_kernel(tc, x, base_weight, spline_weight, spline_scale, gr
         regroup(0)
         quantise(0)
 
-        nxt = {"rg": 1, "q": 1}
+        nxt = {"rg": 1, "q": 1, "mx": 0}
 
         def after_pass(n):
-            if n == 8:
-                scale_v(1, [0, 1, 2, 3])
-                dsilu_a(3)
-                dsilu_b(3)
-            if n == 11:
-                base_quantise()
-            if n == 26:
-                scale_v(2, [0, 1, 2, 3])
             while nxt["rg"] < NT * UPT and regroup_after(nxt["rg"]) <= n:
                 u = nxt["rg"]
                 regroup(u)
@@ -321,19 +320,44 @@ def tile_relukanlayer_kernel(tc, x, base_weight, spline_weight, spline_scale, gr
             while nxt["q"] < len(groups) and quantise_after(nxt["q"]) <= n:
                 quantise(nxt["q"])
                 nxt["q"] += 1
+            if n == 3:
+                scale_v(1, [0, 1])
+            if n == 7:
+                scale_v(1, [2, 3])
+            if n == 11:
+                dsilu_a(3)
+                dsilu_b(3)
+            if n == 15:
+                base_quantise()
+            if n == 26:
+                scale_v(2, [0, 1, 2, 3])
+
+        def ready(r):
+            for n in range(rounds[r][0], rounds[r][1]):
+                it, s = divmod(n, NPASS)
+                if s == G and "base" not in done_rg:
+                    return False
+                if s < G and group_of[it * UPT + s // GU] >= nxt["q"]:
+                    return False
+            return True
+
+        def issue_mx(limit):
+            while nxt["mx"] < len(rounds) and nxt["mx"] <= limit and ready(nxt["mx"]):
+                mx_round(nxt["mx"])
+                nxt["mx"] += 1
 
         after_pass(-1)
-        mx_round(0)
         for r in range(len(rounds)):
+            issue_mx(r + LA)
             if r >= 1:
                 tr_round(r - 1)
                 for n in range(rounds[r - 1][0], rounds[r - 1][1]):
                     if n % NPASS == NPASS - 1:
                         evacuate(n // NPASS)
+            assert nxt["mx"] > r
             for n in range(rounds[r][0], rounds[r][1]):
                 mask(n)
                 after_pass(n)
-            if r + 1 < len(rounds):
-                mx_round(r + 1)
+            issue_mx(r + LA)
         tr_round(len(rounds) - 1)
         evacuate(NT - 1)

@@ -23,8 +23,10 @@ CH = P * G
 GU = 4
 UPT = G // GU
 NPASS = G + 1
-RND = 2
-LA = 2
+RND = 3
+RPT = NPASS // RND
+NR = NT * RPT
+LA_RG = 4
 V_CHUNKS = 3
 
 
@@ -167,7 +169,10 @@ def tile_relukanlayer_kernel(tc, x, base_weight, spline_weight, spline_scale, gr
             off = (u - groups[k][0]) * UW * PACK
             src = raws[it][:].rearrange("p j (i g) -> p i g j", g=G)[:, :, q * GU:(q + 1) * GU, :]
             dst = grps[k][:, off:off + UW * PACK].rearrange("p (g i j) -> p i g j", g=GU, j=PACK)
-            nc.scalar.copy(out=dst, in_=src)
+            if u == 0:
+                nc.vector.tensor_copy(out=dst, in_=src)
+            else:
+                nc.scalar.copy(out=dst, in_=src)
             done_rg.add(u)
 
         def quantise(k):
@@ -180,10 +185,9 @@ def tile_relukanlayer_kernel(tc, x, base_weight, spline_weight, spline_scale, gr
             c, q = divmod(u0, UPT)
             window = None
             if q == 2 and V_CHUNKS <= c + 2 < NT:
-                window = (c + 2, [(0, 0, CH), (1, 0, CH // 2)])
+                window = (c + 2, [(0, 0, CH), (1, 0, CH)])
             if q == 0 and V_CHUNKS <= c + 1 < NT:
-                window = (c + 1, [(1, CH // 2, CH), (2, 0, CH)])
-                scale_v(c + 1, [3])
+                window = (c + 1, [(2, 0, CH), (3, 0, CH)])
             if window is None:
                 nc.vector.quantize_mx(
                     out=cd[:, 0:nu * UW].bitcast(E4M3X4), scales=pl[:, 0:nu * UW], in_=grps[k][:, 0:nu * UW * PACK]
@@ -216,10 +220,9 @@ def tile_relukanlayer_kernel(tc, x, base_weight, spline_weight, spline_scale, gr
 
         def base_quantise():
             nc.vector.quantize_mx(out=b_c[:].bitcast(E4M3X4), scales=b_s[:], in_=bgrp[:])
-            done_rg.add("base")
 
         def mx_round(r):
-            for n in range(rounds[r][0], rounds[r][1]):
+            for n in range(RND * r, RND * r + RND):
                 it, s = divmod(n, NPASS)
                 d = dps.tile([P, B], F32, tag="d", name="d")
                 d_tiles[n] = d
@@ -237,22 +240,23 @@ def tile_relukanlayer_kernel(tc, x, base_weight, spline_weight, spline_scale, gr
                     rhs=gq_c[:].bitcast(E5M2X4), rhs_scale=gq_s[:], start=True, stop=True,
                 )
 
-        def mask(n):
-            it, s = divmod(n, NPASS)
-            t = tp.tile([P, B], F32, name="t")
-            t_tiles[n] = t
-            if s < G:
-                nc.vector.scalar_tensor_tensor(
-                    out=t[:], in0=xT[:, it, :], scalar=grid32[:, s:s + 1], in1=d_tiles[n][:],
-                    op0=ALU.is_gt, op1=ALU.mult,
-                )
-            else:
-                nc.vector.scalar_tensor_tensor(
-                    out=t[:], in0=nds[:, it, :], scalar=-1.0, in1=d_tiles[n][:], op0=ALU.mult, op1=ALU.mult
-                )
+        def t3_round(r):
+            for n in range(RND * r, RND * r + RND):
+                it, s = divmod(n, NPASS)
+                t = tp.tile([P, B], F32, name="t")
+                t_tiles[n] = t
+                if s < G:
+                    nc.vector.scalar_tensor_tensor(
+                        out=t[:], in0=xT[:, it, :], scalar=grid32[:, s:s + 1], in1=d_tiles[n][:],
+                        op0=ALU.is_gt, op1=ALU.mult,
+                    )
+                else:
+                    nc.vector.scalar_tensor_tensor(
+                        out=t[:], in0=nds[:, it, :], scalar=-1.0, in1=d_tiles[n][:], op0=ALU.mult, op1=ALU.mult
+                    )
 
         def tr_round(r):
-            for n in range(rounds[r][0], rounds[r][1]):
+            for n in range(RND * r, RND * r + RND):
                 it, s = divmod(n, NPASS)
                 if s == 0:
                     acc = accp.tile([P, B], F32, name="acc")
@@ -268,26 +272,20 @@ def tile_relukanlayer_kernel(tc, x, base_weight, spline_weight, spline_scale, gr
             nc.scalar.copy(out=osb[:].rearrange("p t i -> p (t i)"), in_=accs[it][:])
             nc.sync.dma_start(out=out_view[:, :, it * P:(it + 1) * P], in_=osb[:])
 
-        def first_pass(u):
+        def first_round(u):
             it, q = divmod(u, UPT)
-            return it * NPASS + q * GU
+            return it * RPT + (q * GU) // RND
 
-        NP = NT * NPASS
-        rounds = [(a, a + RND) for a in range(0, NP, RND)]
-
-        def quantise_after(k):
+        def slot(k):
             u0 = groups[k][0]
-            c, q = divmod(u0, UPT)
-            if c == 0:
-                return first_pass(u0) - 1
-            if c == 1:
-                return first_pass(u0) - (3 if q == 0 else 7)
-            return first_pass(u0) - (10 - q // 2)
+            if u0 < 3:
+                return first_round(u0) - 1
+            return first_round(u0) - 2 - (1 if u0 % UPT == 0 and u0 >= 2 * UPT else 0)
 
-        def regroup_after(u):
-            if u < UPT:
-                return first_pass(u) - 12
-            return first_pass(u) - (13 if u < 2 * UPT else 15)
+        def last_group(r):
+            n = min(RND * r + RND - 1, NT * NPASS - 1)
+            it, s = divmod(n, NPASS)
+            return group_of[it * UPT + min(s, G - 1) // GU]
 
         x_transposes(0)
         x_transposes(1)
@@ -303,61 +301,44 @@ def tile_relukanlayer_kernel(tc, x, base_weight, spline_weight, spline_scale, gr
         scale_v(0, [3])
         dsilu_b(1)
         nc.vector.quantize_mx(out=gq_c[:].bitcast(E5M2X4), scales=gq_s[:], in_=gg[:])
-        dsilu_a(2)
-        dsilu_b(2)
         regroup(0)
         quantise(0)
 
-        nxt = {"rg": 1, "q": 1, "mx": 0}
-
-        def after_pass(n):
-            while nxt["rg"] < NT * UPT and regroup_after(nxt["rg"]) <= n:
+        nxt = {"rg": 1, "q": 1}
+        for r in range(-1, NR + 1):
+            if r == 8:
+                scale_v(2, [0, 1, 2, 3])
+            while nxt["rg"] < NT * UPT and first_round(nxt["rg"]) - LA_RG <= r:
                 u = nxt["rg"]
                 regroup(u)
                 if u % UPT == UPT - 1 and u // UPT + 4 < NT:
                     load_chunk(u // UPT + 4)
                 nxt["rg"] += 1
-            while nxt["q"] < len(groups) and quantise_after(nxt["q"]) <= n:
-                quantise(nxt["q"])
-                nxt["q"] += 1
-            if n == 3:
-                scale_v(1, [0, 1])
-            if n == 7:
-                scale_v(1, [2, 3])
-            if n == 11:
-                dsilu_a(3)
-                dsilu_b(3)
-            if n == 15:
-                base_quantise()
-            if n == 26:
-                scale_v(2, [0, 1, 2, 3])
-
-        def ready(r):
-            for n in range(rounds[r][0], rounds[r][1]):
-                it, s = divmod(n, NPASS)
-                if s == G and "base" not in done_rg:
-                    return False
-                if s < G and group_of[it * UPT + s // GU] >= nxt["q"]:
-                    return False
-            return True
-
-        def issue_mx(limit):
-            while nxt["mx"] < len(rounds) and nxt["mx"] <= limit and ready(nxt["mx"]):
-                mx_round(nxt["mx"])
-                nxt["mx"] += 1
-
-        after_pass(-1)
-        for r in range(len(rounds)):
-            issue_mx(r + LA)
+            early = r + 1 < NR and last_group(r + 1) < nxt["q"]
+            if early:
+                mx_round(r + 1)
             if r >= 1:
                 tr_round(r - 1)
-                for n in range(rounds[r - 1][0], rounds[r - 1][1]):
-                    if n % NPASS == NPASS - 1:
-                        evacuate(n // NPASS)
-            assert nxt["mx"] > r
-            for n in range(rounds[r][0], rounds[r][1]):
-                mask(n)
-                after_pass(n)
-            issue_mx(r + LA)
-        tr_round(len(rounds) - 1)
-        evacuate(NT - 1)
+            if 0 <= r < NR:
+                t3_round(r)
+            while nxt["q"] < len(groups) and (
+                slot(nxt["q"]) <= r or (r + 1 < NR and nxt["q"] <= last_group(r + 1))
+            ):
+                quantise(nxt["q"])
+                nxt["q"] += 1
+            if r + 1 < NR and not early:
+                mx_round(r + 1)
+            if r == 0:
+                scale_v(1, [0, 1])
+            if r == 1:
+                scale_v(1, [2, 3])
+            if r == 9:
+                dsilu_a(2)
+                dsilu_b(2)
+            if r == 16:
+                dsilu_a(3)
+                dsilu_b(3)
+            if r == 3:
+                base_quantise()
+            if r >= 1 and (r - 1) % RPT == RPT - 1:
+                evacuate((r - 1) // RPT)

from contextlib import ExitStack

import concourse.mybir as mybir
from concourse.masks import make_identity

BF16 = mybir.dt.bfloat16
F32 = mybir.dt.float32
U32 = mybir.dt.uint32
U8 = mybir.dt.uint8
E4M3X4 = mybir.dt.float8_e4m3fn_x4
E5M2X4 = mybir.dt.float8_e5m2_x4
ALU = mybir.AluOpType
ACT = mybir.ActivationFunctionType

P = 128
B, IN, OUT, G = 512, 1024, 512, 20
PACK = 4
FLOPS = 2 * B * OUT * (IN + IN * G)

NT = IN // P
NBT = B // P
CH = P * G
GU = 4
UPT = G // GU
NPASS = G + 1
RND = 3
RPT = NPASS // RND
NR = NT * RPT
LA_RG = 4
V_CHUNKS = 3


def tile_relukanlayer_kernel(tc, x, base_weight, spline_weight, spline_scale, grid, grad_out, out):
    nc = tc.nc
    with ExitStack() as ctx:
        const = ctx.enter_context(tc.tile_pool(name="const", bufs=1))
        rawp = ctx.enter_context(tc.tile_pool(name="rawp", bufs=4))
        grpp = ctx.enter_context(tc.tile_pool(name="grpp", bufs=3))
        cdp = ctx.enter_context(tc.tile_pool(name="cdp", bufs=4))
        tp = ctx.enter_context(tc.tile_pool(name="tp", bufs=8))
        wkp = ctx.enter_context(tc.tile_pool(name="wkp", bufs=1))
        flp = ctx.enter_context(tc.tile_pool(name="flp", bufs=2))
        osp = ctx.enter_context(tc.tile_pool(name="osp", bufs=2))
        dps = ctx.enter_context(tc.psum_pool(name="dps", bufs=6))
        accp = ctx.enter_context(tc.psum_pool(name="accp", bufs=2))
        ctx.enter_context(tc.manual_schedule())

        w_view = spline_weight.rearrange("(p j) i g -> p j (i g)", j=PACK)
        out_view = out.rearrange("(t p) i -> p t i", p=P)

        raws = {}
        codes = {}
        planes = {}
        d_tiles = {}
        t_tiles = {}
        accs = {}

        def load_chunk(c):
            raw = rawp.tile([P, PACK, CH], BF16, name="raw")
            raws[c] = raw
            for j in range(PACK):
                nc.sync.dma_start(out=raw[:, j, :], in_=w_view[:, j, c * CH:(c + 1) * CH])

        s_bf = const.tile([P, PACK], BF16, name="s_bf")
        nc.scalar.dma_start(out=s_bf[:], in_=spline_scale.rearrange("(p j) a c -> p (j a c)", j=PACK))
        grid_bf = const.tile([P, G], BF16, name="grid_bf")
        nc.scalar.dma_start(out=grid_bf[:], in_=grid.partition_broadcast(P))
        x_sb = const.tile([P, NBT, IN], BF16, name="x_sb")
        nc.sync.dma_start(out=x_sb[:], in_=x.rearrange("(t p) i -> p t i", p=P))
        g_sb = const.tile([P, NBT, OUT], BF16, name="g_sb")
        nc.sync.dma_start(out=g_sb[:], in_=grad_out.rearrange("(t p) o -> p t o", p=P))
        load_chunk(0)
        rawb = const.tile([P, PACK, IN], BF16, name="rawb")
        nc.sync.dma_start(out=rawb[:], in_=base_weight.rearrange("(p j) i -> p j i", j=PACK))
        load_chunk(1)
        load_chunk(2)
        load_chunk(3)

        ident_b = const.tile([P, P], BF16, name="ident_b")
        make_identity(nc, ident_b[:])
        ident_f = const.tile([P, P], F32, name="ident_f")
        make_identity(nc, ident_f[:])

        s32 = const.tile([P, PACK], F32, name="s32")
        nc.vector.tensor_copy(out=s32[:], in_=s_bf[:])
        grid32 = const.tile([P, G], F32, name="grid32")
        nc.vector.tensor_copy(out=grid32[:], in_=grid_bf[:])

        xT = const.tile([P, NT, B], BF16, name="xT")
        sg = const.tile([P, NT, B], F32, name="sg")
        nds = const.tile([P, NT, B], F32, name="nds")

        def x_transposes(k):
            xp = dps.tile([P, 2, B], BF16, tag="d", name="xp")
            for h in range(2):
                for t in range(NBT):
                    nc.tensor.transpose(
                        xp[:, h, t * P:(t + 1) * P], x_sb[:, t, (2 * k + h) * P:(2 * k + h + 1) * P], ident_b[:]
                    )
            nc.scalar.copy(out=xT[:, 2 * k:2 * k + 2, :], in_=xp[:])
            nc.scalar.activation(out=sg[:, 2 * k:2 * k + 2, :], in_=xT[:, 2 * k:2 * k + 2, :], func=ACT.Sigmoid)

        tqs = {}

        def dsilu_a(k):
            sl = slice(2 * k, 2 * k + 2)
            tq = wkp.tile([P, 2, B], F32, name="tq")
            tqs[k] = tq
            nc.vector.scalar_tensor_tensor(
                out=tq[:], in0=sg[:, sl, :], scalar=1.0, in1=xT[:, sl, :], op0=ALU.subtract, op1=ALU.mult
            )

        def dsilu_b(k):
            sl = slice(2 * k, 2 * k + 2)
            nc.vector.scalar_tensor_tensor(
                out=nds[:, sl, :], in0=tqs[k][:], scalar=1.0, in1=sg[:, sl, :], op0=ALU.subtract, op1=ALU.mult
            )

        gg = const.tile([P, PACK * B], BF16, name="gg", align_bytes=64)
        gq_c = const.tile([P, B], U32, name="gq_c", align_bytes=64)
        gq_s = const.tile([P, B], U8, name="gq_s", align_bytes=64)

        def g_transposes():
            for h in range(2):
                gp = dps.tile([P, 2, 2 * P], F32, tag="d", name="gp")
                for u in range(2):
                    for tt in range(2):
                        words = g_sb[:, 2 * h + tt, :].bitcast(F32).rearrange("p (q u) -> p q u", u=2)[:, :, u]
                        nc.tensor.transpose(gp[:, u, tt * P:(tt + 1) * P], words, ident_f[:])
                nc.scalar.copy(
                    out=gg[:].bitcast(F32)[:, h * 4 * P:(h + 1) * 4 * P].rearrange("p (b u) -> p b u", u=2),
                    in_=gp[:].rearrange("p u b -> p b u"),
                )

        def scale_v(c, js):
            raw = raws[c]
            for j in js:
                nc.vector.tensor_scalar(
                    out=raw[:, j, :], in0=raw[:, j, :], scalar1=s32[:, j:j + 1], scalar2=None, op0=ALU.mult
                )

        def scale_g(c, pieces):
            raw = raws[c]
            fl = flp.tile([P, 1], F32, name="fl")
            nc.vector.memset(fl[:], 0.0)
            for n, (j, lo, hi) in enumerate(pieces):
                nc.gpsimd.tensor_scalar(
                    out=raw[:, j, lo:hi], in0=raw[:, j, lo:hi], scalar1=s32[:, j:j + 1],
                    scalar2=(fl[:, 0:1] if n == 0 else 0.0), op0=ALU.mult, op1=ALU.add,
                )

        groups = [(u, 1) for u in range(UPT)]
        for c in range(1, NT):
            groups.extend([(c * UPT, 2), (c * UPT + 2, 2), (c * UPT + 4, 1)])
        group_of = {}
        for k, (u0, nu) in enumerate(groups):
            for u in range(u0, u0 + nu):
                group_of[u] = k
        UW = GU * P
        grps = {}
        done_rg = set()

        def regroup(u):
            it, q = divmod(u, UPT)
            k = group_of[u]
            if u == groups[k][0]:
                grp = grpp.tile([P, 2 * UW * PACK], BF16, name="grp", align_bytes=64)
                grps[k] = grp
            off = (u - groups[k][0]) * UW * PACK
            src = raws[it][:].rearrange("p j (i g) -> p i g j", g=G)[:, :, q * GU:(q + 1) * GU, :]
            dst = grps[k][:, off:off + UW * PACK].rearrange("p (g i j) -> p i g j", g=GU, j=PACK)
            if u == 0:
                nc.vector.tensor_copy(out=dst, in_=src)
            else:
                nc.scalar.copy(out=dst, in_=src)
            done_rg.add(u)

        def quantise(k):
            u0, nu = groups[k]
            assert all(u in done_rg for u in range(u0, u0 + nu))
            cd = cdp.tile([P, 2 * UW], U32, name="cd", align_bytes=64)
            pl = cdp.tile([P, 2 * UW], U8, name="pl", align_bytes=64)
            codes[k] = cd
            planes[k] = pl
            c, q = divmod(u0, UPT)
            window = None
            if q == 2 and V_CHUNKS <= c + 2 < NT:
                window = (c + 2, [(0, 0, CH), (1, 0, CH)])
            if q == 0 and V_CHUNKS <= c + 1 < NT:
                window = (c + 1, [(2, 0, CH), (3, 0, CH)])
            if window is None:
                nc.vector.quantize_mx(
                    out=cd[:, 0:nu * UW].bitcast(E4M3X4), scales=pl[:, 0:nu * UW], in_=grps[k][:, 0:nu * UW * PACK]
                )
                if k < 4:
                    base_regroup(k)
            else:
                for h in range(2):
                    nc.vector.quantize_mx(
                        out=cd[:, h * UW:(h + 1) * UW].bitcast(E4M3X4), scales=pl[:, h * UW:(h + 1) * UW],
                        in_=grps[k][:, h * UW * PACK:(h + 1) * UW * PACK],
                    )
                    if h == 0:
                        scale_g(window[0], window[1])

        bgrp = const.tile([P, IN * PACK], BF16, name="bgrp", align_bytes=64)
        b_c = const.tile([P, IN], U32, name="b_c", align_bytes=64)
        b_s = const.tile([P, IN], U8, name="b_s", align_bytes=64)

        BW = IN // 4

        def base_regroup(m):
            fl = flp.tile([P, 1], F32, name="fl")
            nc.vector.memset(fl[:], 0.0)
            nc.gpsimd.tensor_scalar(
                out=bgrp[:, m * BW * PACK:(m + 1) * BW * PACK].rearrange("p (w j) -> p w j", j=PACK),
                in0=rawb[:, :, m * BW:(m + 1) * BW].rearrange("p j w -> p w j"),
                scalar1=1.0, scalar2=fl[:, 0:1], op0=ALU.mult, op1=ALU.add,
            )

        def base_quantise():
            nc.vector.quantize_mx(out=b_c[:].bitcast(E4M3X4), scales=b_s[:], in_=bgrp[:])

        def mx_round(r):
            for n in range(RND * r, RND * r + RND):
                it, s = divmod(n, NPASS)
                d = dps.tile([P, B], F32, tag="d", name="d")
                d_tiles[n] = d
                if s < G:
                    u = it * UPT + s // GU
                    k = group_of[u]
                    c0 = (u - groups[k][0]) * UW + (s % GU) * P
                    cols = slice(c0, c0 + P)
                    lhsT, lhsT_scale = codes[k][:, cols], planes[k][:, cols]
                else:
                    cols = slice(it * P, (it + 1) * P)
                    lhsT, lhsT_scale = b_c[:, cols], b_s[:, cols]
                nc.tensor.matmul_mx(
                    out=d[:], lhsT=lhsT.bitcast(E4M3X4), lhsT_scale=lhsT_scale,
                    rhs=gq_c[:].bitcast(E5M2X4), rhs_scale=gq_s[:], start=True, stop=True,
                )

        def t3_round(r):
            for n in range(RND * r, RND * r + RND):
                it, s = divmod(n, NPASS)
                t = tp.tile([P, B], F32, name="t")
                t_tiles[n] = t
                if s < G:
                    nc.vector.scalar_tensor_tensor(
                        out=t[:], in0=xT[:, it, :], scalar=grid32[:, s:s + 1], in1=d_tiles[n][:],
                        op0=ALU.is_gt, op1=ALU.mult,
                    )
                else:
                    nc.vector.scalar_tensor_tensor(
                        out=t[:], in0=nds[:, it, :], scalar=-1.0, in1=d_tiles[n][:], op0=ALU.mult, op1=ALU.mult
                    )

        def tr_round(r):
            for n in range(RND * r, RND * r + RND):
                it, s = divmod(n, NPASS)
                if s == 0:
                    acc = accp.tile([P, B], F32, name="acc")
                    accs[it] = acc
                for bt in range(NBT):
                    nc.tensor.matmul(
                        out=accs[it][:, bt * P:(bt + 1) * P], lhsT=t_tiles[n][:, bt * P:(bt + 1) * P], rhs=ident_f[:],
                        is_transpose=True, start=(s == 0 and bt == 0), stop=(s == NPASS - 1 and bt == NBT - 1),
                    )

        def evacuate(it):
            osb = osp.tile([P, NBT, P], F32, name="osb")
            nc.scalar.copy(out=osb[:].rearrange("p t i -> p (t i)"), in_=accs[it][:])
            nc.sync.dma_start(out=out_view[:, :, it * P:(it + 1) * P], in_=osb[:])

        def first_round(u):
            it, q = divmod(u, UPT)
            return it * RPT + (q * GU) // RND

        def slot(k):
            u0 = groups[k][0]
            if u0 < 3:
                return first_round(u0) - 1
            return first_round(u0) - 2 - (1 if u0 % UPT == 0 and u0 >= 2 * UPT else 0)

        def last_group(r):
            n = min(RND * r + RND - 1, NT * NPASS - 1)
            it, s = divmod(n, NPASS)
            return group_of[it * UPT + min(s, G - 1) // GU]

        x_transposes(0)
        x_transposes(1)
        g_transposes()
        x_transposes(2)
        x_transposes(3)
        scale_v(0, [0])
        dsilu_a(0)
        scale_v(0, [1])
        dsilu_b(0)
        scale_v(0, [2])
        dsilu_a(1)
        scale_v(0, [3])
        dsilu_b(1)
        nc.vector.quantize_mx(out=gq_c[:].bitcast(E5M2X4), scales=gq_s[:], in_=gg[:])
        regroup(0)
        quantise(0)

        nxt = {"rg": 1, "q": 1}
        for r in range(-1, NR + 1):
            if r == 8:
                scale_v(2, [0, 1, 2, 3])
            while nxt["rg"] < NT * UPT and first_round(nxt["rg"]) - LA_RG <= r:
                u = nxt["rg"]
                regroup(u)
                if u % UPT == UPT - 1 and u // UPT + 4 < NT:
                    load_chunk(u // UPT + 4)
                nxt["rg"] += 1
            early = r + 1 < NR and last_group(r + 1) < nxt["q"]
            if early:
                mx_round(r + 1)
            if r >= 1:
                tr_round(r - 1)
            if 0 <= r < NR:
                t3_round(r)
            while nxt["q"] < len(groups) and (
                slot(nxt["q"]) <= r or (r + 1 < NR and nxt["q"] <= last_group(r + 1))
            ):
                quantise(nxt["q"])
                nxt["q"] += 1
            if r + 1 < NR and not early:
                mx_round(r + 1)
            if r == 0:
                scale_v(1, [0, 1])
            if r == 1:
                scale_v(1, [2, 3])
            if r == 9:
                dsilu_a(2)
                dsilu_b(2)
            if r == 16:
                dsilu_a(3)
                dsilu_b(3)
            if r == 3:
                base_quantise()
            if r >= 1 and (r - 1) % RPT == RPT - 1:
                evacuate((r - 1) // RPT)
